import numpy as np
import ml_dtypes


def mxq(x, axis, fmt="e4m3"):
    dtype, down = {"e4m3": (ml_dtypes.float8_e4m3fn, 7), "e5m2": (ml_dtypes.float8_e5m2, 14)}[fmt]
    v = np.moveaxis(np.asarray(x, np.float32).astype(ml_dtypes.bfloat16).astype(np.float64), axis, -1)
    blocks = v.reshape(v.shape[:-1] + (-1, 32))
    amax = np.abs(blocks).max(-1, keepdims=True)
    byte = np.maximum(np.where(amax > 0, np.frexp(amax)[1] - 1 + 127, 0) - down, 1)
    scale = np.exp2(byte - 127.0)
    codes = (blocks / scale).astype(np.float32).astype(dtype).astype(np.float64)
    return np.moveaxis((codes * scale).reshape(v.shape), -1, axis)


WIDE = False


def mx_kscale(k):
    if not WIDE:
        return np.ones(k)
    levels = np.array([10, -10, 5, -5, 0])
    if k % 512:
        return np.exp2(np.random.permutation(np.resize(levels, k // 32))).repeat(32)
    a = np.empty((k // 512, 16))
    for p in range(k // 512):
        a[p, :8] = np.random.permutation(np.resize(levels, 8))
        for g in range(8):
            far = levels[np.abs(levels - a[p, g]) >= 10]
            a[p, g + 8] = far[np.random.randint(len(far))]
    return np.exp2(a.ravel()).repeat(32)


BF16 = ml_dtypes.bfloat16


def bf(x):
    return np.asarray(x, np.float32).astype(BF16)


def f64(x):
    return np.asarray(x).astype(np.float64)


B, N, C0, C1, C2, O0, O1, O2 = 16, 16, 512, 512, 512, 512, 2048, 512
G = C1 + C2
K = 2 * G
T = B * N * N


def sigmoid(v):
    return 1.0 / (1.0 + np.exp(-v))


def preact(x1, x2, W2, b2):
    x1, x2 = f64(x1), f64(x2)
    e1 = np.broadcast_to(x1[:, :, None, :], (B, N, N, C1))
    g = np.concatenate([e1, x2], axis=-1)
    f2 = np.concatenate([g, np.swapaxes(g, 1, 2)], axis=-1)
    return f2 @ f64(W2) + f64(b2)


def setup_inputs():
    s = mx_kscale(T).reshape(B, N * N)[:, 0]
    u = mx_kscale(O2)
    x10 = bf(np.random.random((B, N, C1)))
    x20 = bf(np.random.random((B, N, N, C2)))
    W20 = bf(np.random.standard_normal((K, O2)) * 2.0 / np.sqrt(K))
    b2 = bf(np.random.standard_normal(O2) * 0.3)
    g = bf(np.random.standard_normal((B, N, N, O2)) * np.exp2(np.random.randint(-6, 1, (B, N, N, 1))) * 4.0
           / s[:, None, None, None] * u)
    z = preact(x10, x20, W20, b2)
    return {"x1": bf(f64(x10) * s[:, None, None]), "x2": bf(f64(x20) * s[:, None, None, None]),
            "W2": bf(f64(W20) / u[None, :]), "b2": b2,
            "z": np.asarray(z, np.float32), "grad_out": g}


def reference(x1, x2, W2, b2, z, grad_out):
    sg = sigmoid(f64(z))
    dz4 = f64(grad_out) * (sg * (1.0 - sg))
    dz = dz4.reshape(T, O2)
    W = f64(W2)
    v = np.concatenate([W[C1:G], W[G + C1:K]], axis=0)
    p = (mxq(dz, 1, "e5m2") @ mxq(v, 1, "e4m3").T).reshape(B, N, N, 2 * C2)
    dx2 = p[..., :C2] + np.swapaxes(p[..., C2:], 1, 2)
    xx = f64(x2)
    h = np.concatenate([xx, np.swapaxes(xx, 1, 2)], axis=-1).reshape(T, 2 * C2)
    m = mxq(h, 0, "e4m3").T @ mxq(dz, 0, "e5m2")
    x1f = f64(x1).reshape(B * N, C1)
    da = x1f.T @ dz4.sum(axis=2).reshape(B * N, O2)
    dc = x1f.T @ dz4.sum(axis=1).reshape(B * N, O2)
    dW2 = np.concatenate([da, m[:C2], dc, m[C2:]], axis=0)
    return dx2, dW2

@@ -1,0 +1,249 @@
+from contextlib import ExitStack
+
+import concourse.mybir as mybir
+from concourse.masks import make_block_diagonal, make_identity
+
+F32 = mybir.dt.float32
+BF16 = mybir.dt.bfloat16
+U32 = mybir.dt.uint32
+U8 = mybir.dt.uint8
+E4 = mybir.dt.float8_e4m3fn_x4
+E5 = mybir.dt.float8_e5m2_x4
+ACT = mybir.ActivationFunctionType
+ALU = mybir.AluOpType
+
+FLOPS = 2 * (2 * 4096 * 512 * 1024) + 2 * (2 * 256 * 512 * 512)
+
+P = 128
+W = 512
+NPASS = 8
+
+
+def tile_differentiablelogicmachine_pa_v_kernel(tc, x1, x2, W2, b2, z, grad_out, out_0, out_1):
+    nc = tc.nc
+
+    z_v = z.rearrange("b (m e) (k j) o -> m e b k (j o)", e=2, j=2)
+    g_v = grad_out.rearrange("b (m e) (k j) o -> m e b k (j o)", e=2, j=2)
+    x2_v = x2.rearrange("b (m e) (k j) o -> m e b k (j o)", e=2, j=2)
+    x2s_v = x2.rearrange("b (k j) i c -> (b k) j i c", j=2)
+    x1a_v = x1.rearrange("b (q v) c -> q b v c", v=8)
+    x1b_v = x1.rearrange("b (k j) c -> j (b k) c", j=2)
+    out0_v = out_0.rearrange("b i j c -> (b i j) c")
+
+    def load_pass(tile, view, m):
+        for e in (0, 1):
+            nc.sync.dma_start(
+                out=tile[:, 2 * e : 2 * e + 2, :].rearrange("p t o -> p (t o)"), in_=view[m, e]
+            )
+
+    with ExitStack() as ctx:
+        const = ctx.enter_context(tc.tile_pool(name="const", bufs=1))
+        ident = const.tile([P, P], F32, name="ident", tag="ident")
+        bm = const.tile([P, P], F32, name="bm", tag="bm")
+        cio = const.tile([P, P], F32, name="cio", tag="cio")
+        sel_a = const.tile([P, 8, P], F32, name="sel_a", tag="sel_a")
+        x1a = const.tile([P, 2, W], F32, name="x1a", tag="x1a")
+        x1b = const.tile([P, 2, W], F32, name="x1b", tag="x1b")
+        vq = const.tile([P, 1024], U32, name="vq", tag="vq", align_bytes=64)
+        vs = const.tile([P, 1024], U8, name="vs", tag="vs", align_bytes=64)
+        dzq = const.tile([P, NPASS, W], U32, name="dzq", tag="dzq", align_bytes=64)
+        dzs = const.tile([P, NPASS, W], U8, name="dzs", tag="dzs", align_bytes=64)
+        nst = const.tile([P, 4096 * 4], BF16, name="nst", tag="nst", align_bytes=64)
+        p_b = const.tile([P, 2, W], F32, name="p_b", tag="p_b")
+        s_a = const.tile([P, 2, W], F32, name="s_a", tag="s_a")
+        warm = const.tile([P, 1], F32, name="warm", tag="warm")
+
+        nc.vector.memset(warm[:], 0.0)
+        nc.scalar.activation(out=warm[:], in_=warm[:], func=ACT.Sigmoid)
+
+        make_identity(nc, ident[:])
+        make_block_diagonal(nc, bm[:], 8)
+        nc.gpsimd.iota(
+            cio[:], pattern=[[0, 16], [1, 8]], base=0, channel_multiplier=0, allow_small_or_imprecise_dtypes=True
+        )
+        for v in range(8):
+            nc.vector.scalar_tensor_tensor(
+                out=sel_a[:, v, :], in0=cio[:], scalar=float(v), in1=bm[:], op0=ALU.is_equal, op1=ALU.mult
+            )
+
+        nw = nst[:].bitcast(F32)
+        n_v = nw.rearrange("p (b m e k x) -> p m e b k x", b=16, m=NPASS, e=2, k=8, x=4)
+
+        with tc.tile_pool(name="vprep", bufs=1) as vp, tc.psum_pool(name="psv", bufs=2) as psv:
+            wraw = vp.tile([P, 8, W], BF16, name="wraw", tag="wraw")
+            for s in (0, 1):
+                nc.sync.dma_start(
+                    out=wraw[:, 4 * s : 4 * s + 4, :],
+                    in_=W2[512 + 1024 * s : 1024 + 1024 * s, :].rearrange("(r p) o -> p r o", p=P),
+                )
+            x1ar = vp.tile([P, 2, W], BF16, name="x1ar", tag="x1ar")
+            x1br = vp.tile([P, 2, W], BF16, name="x1br", tag="x1br")
+            for q in (0, 1):
+                nc.sync.dma_start(out=x1ar[:, q, :], in_=x1a_v[q])
+                nc.sync.dma_start(out=x1br[:, q, :], in_=x1b_v[q])
+            nc.vector.tensor_copy(out=x1a[:], in_=x1ar[:])
+            nc.vector.tensor_copy(out=x1b[:], in_=x1br[:])
+
+            vgrp = vp.tile([P, 4096], BF16, name="vgrp", tag="vgrp", align_bytes=64)
+            vgw = vgrp[:].bitcast(F32)
+            for a2 in range(4):
+                vps = psv.tile([P, 2, 2, P], F32, name="vps", tag="vps")
+                for a in (0, 1):
+                    words = wraw[:, 2 * a2 + a, :].bitcast(F32)
+                    for u in (0, 1):
+                        nc.tensor.transpose(vps[:, a, u, :], words[:, u:256:2], ident[:])
+                nc.vector.tensor_copy(
+                    out=vgw[:, 512 * a2 : 512 * (a2 + 1)].rearrange("p (a r u) -> p a r u", a=2, u=2),
+                    in_=vps[:].rearrange("p a u r -> p a r u"),
+                )
+            nc.vector.quantize_mx(out=vq[:].bitcast(E4), scales=vs[:], in_=vgrp[:])
+
+        late = ctx.enter_context(tc.tile_pool(name="late", bufs=2))
+        ostp = ctx.enter_context(tc.tile_pool(name="ostp", bufs=4))
+        zp = ctx.enter_context(tc.tile_pool(name="zp", bufs=3))
+        wk = ctx.enter_context(tc.tile_pool(name="wk", bufs=2))
+        grpp = ctx.enter_context(tc.tile_pool(name="grpp", bufs=3))
+        cdp = ctx.enter_context(tc.tile_pool(name="cdp", bufs=3))
+
+        with tc.psum_pool(name="ps1", bufs=2) as ps1:
+            sa_ps = None
+            for m in range(NPASS):
+                zt = zp.tile([P, 4, W], F32, name="zt", tag="zt")
+                gt = zp.tile([P, 4, W], BF16, name="gt", tag="gt")
+                load_pass(zt, z_v, m)
+                load_pass(gt, g_v, m)
+                dzb = wk.tile([P, 4, W], BF16, name="dzb", tag="dzb")
+                pa = wk.tile([P, 2, W], F32, name="pa", tag="pa")
+                for e in (0, 1):
+                    ze = zt[:, 2 * e : 2 * e + 2, :]
+                    nc.scalar.activation(out=ze, in_=ze, func=ACT.Sigmoid)
+                    nc.scalar.activation(out=ze, in_=ze, func=ACT.Square, bias=-0.5)
+                    nc.vector.scalar_tensor_tensor(
+                        out=ze, in0=ze, scalar=0.25, in1=gt[:, 2 * e : 2 * e + 2, :], op0=ALU.subtract, op1=ALU.mult
+                    )
+                    nc.scalar.copy(out=dzb[:, 2 * e : 2 * e + 2, :], in_=ze)
+                    nc.vector.tensor_tensor(
+                        out=pa[:, e, :], in0=zt[:, 2 * e, :], in1=zt[:, 2 * e + 1, :], op=ALU.add
+                    )
+                if m == 0:
+                    nc.vector.tensor_tensor(out=p_b[:], in0=zt[:, 0:2, :], in1=zt[:, 2:4, :], op=ALU.add)
+                else:
+                    tb = wk.tile([P, 2, W], F32, name="tb", tag="tb")
+                    nc.vector.tensor_tensor(out=tb[:], in0=zt[:, 0:2, :], in1=zt[:, 2:4, :], op=ALU.add)
+                    nc.vector.tensor_tensor(out=p_b[:], in0=p_b[:], in1=tb[:], op=ALU.add)
+
+                grp = grpp.tile([P, W, 4], BF16, name="grp", tag="grp", align_bytes=64)
+                nc.vector.tensor_copy(out=grp[:], in_=dzb[:].rearrange("p t o -> p o t"))
+                nc.vector.quantize_mx(
+                    out=dzq[:, m, :].bitcast(E5), scales=dzs[:, m, :], in_=grp[:].rearrange("p o t -> p (o t)")
+                )
+
+                dzw = dzb[:].bitcast(F32)
+                for e in (0, 1):
+                    tps = ps1.tile([P, 4, P], F32, name="tps", tag="tps", bufs=3)
+                    for jl in (0, 1):
+                        for u in (0, 1):
+                            nc.tensor.transpose(tps[:, 2 * jl + u, :], dzw[:, 2 * e + jl, u:256:2], ident[:])
+                    nc.scalar.copy(out=n_v[:, m, e], in_=tps[:].rearrange("p x (b k) -> p b k x", k=8))
+
+                if m % 4 == 0:
+                    sa_ps = ps1.tile([P, W], F32, name="sa_ps", tag="sa_ps", bufs=2)
+                for e in (0, 1):
+                    v = 2 * (m % 4) + e
+                    nc.tensor.matmul(
+                        out=sa_ps[:], lhsT=sel_a[:, v, :], rhs=pa[:, e, :], start=(v == 0), stop=(v == 7)
+                    )
+                if m % 4 == 3:
+                    nc.vector.tensor_copy(out=s_a[:, m // 4, :], in_=sa_ps[:])
+
+        with tc.psum_pool(name="ps2", bufs=2) as ps2, tc.psum_pool(name="psm", bufs=1) as psm:
+            xs = []
+            for hm in (0, 1):
+                xst = late.tile([P, 2, 8, W], BF16, name="xst", tag="xst")
+                nc.sync.dma_start(out=xst[:], in_=x2s_v[:, :, 8 * hm : 8 * hm + 8, :])
+                xs.append(xst)
+
+            def small_product(n):
+                cc = n % 4
+                acc = ps2.tile([P, W], F32, name="dd", tag="dd")
+                for q in (0, 1):
+                    if n < 4:
+                        nc.tensor.matmul(
+                            out=acc[:], lhsT=x1a[:, q, P * cc : P * (cc + 1)], rhs=s_a[:, q, :], start=(q == 0), stop=(q == 1)
+                        )
+                    else:
+                        nc.tensor.matmul(
+                            out=acc[:], lhsT=x1b[:, q, P * cc : P * (cc + 1)], rhs=p_b[:, q, :], start=(q == 0), stop=(q == 1)
+                        )
+                o1 = late.tile([P, W], F32, name="o1", tag="o1")
+                nc.scalar.activation(out=o1[:], in_=acc[:], func=ACT.Copy, scale=-1.0)
+                r0 = P * cc + (0 if n < 4 else 1024)
+                nc.scalar.dma_start(out=out_1[r0 : r0 + P, :], in_=o1[:])
+
+            def p_chunk(c):
+                nq = cdp.tile([P, W], U32, name="nq", tag="nq", bufs=2, align_bytes=64)
+                nqs = cdp.tile([P, W], U8, name="nqs", tag="nqs", bufs=2, align_bytes=64)
+                nc.vector.quantize_mx(out=nq[:].bitcast(E5), scales=nqs[:], in_=nst[:, 2048 * c : 2048 * (c + 1)])
+                sst = late.tile([P, 2048], BF16, name="sst", tag="sst", align_bytes=64)
+                for sc in (0, 1):
+                    b = 2 * c + sc
+                    nc.vector.tensor_copy(
+                        out=sst[:, 1024 * sc : 1024 * (sc + 1)].rearrange("p (i j t) -> p i j t", i=16, j=16),
+                        in_=nst[:, 1024 * b : 1024 * (b + 1)].rearrange("p (j i t) -> p i j t", i=16, j=16),
+                    )
+                sq = cdp.tile([P, W], U32, name="sq", tag="sq", bufs=2, align_bytes=64)
+                sqs = cdp.tile([P, W], U8, name="sqs", tag="sqs", bufs=2, align_bytes=64)
+                nc.vector.quantize_mx(out=sq[:].bitcast(E5), scales=sqs[:], in_=sst[:])
+                for a in range(4):
+                    cols = slice(P * a, P * (a + 1))
+                    acc = ps2.tile([P, W], F32, name="pp", tag="pp")
+                    nc.tensor.matmul_mx(
+                        out=acc[:], lhsT=nq[:, cols].bitcast(E5), lhsT_scale=nqs[:, cols],
+                        rhs=vq[:, 0:512].bitcast(E4), rhs_scale=vs[:, 0:512], start=True, stop=False,
+                    )
+                    nc.tensor.matmul_mx(
+                        out=acc[:], lhsT=sq[:, cols].bitcast(E5), lhsT_scale=sqs[:, cols],
+                        rhs=vq[:, 512:1024].bitcast(E4), rhs_scale=vs[:, 512:1024], start=False, stop=True,
+                    )
+                    ost = ostp.tile([P, W], F32, name="ost", tag="ost")
+                    nc.scalar.activation(out=ost[:], in_=acc[:], func=ACT.Copy, scale=-1.0)
+                    r0 = 512 * c + P * a
+                    nc.scalar.dma_start(out=out0_v[r0 : r0 + P, :], in_=ost[:])
+
+            for half in (0, 1):
+                maccs = []
+                for a in range(4):
+                    macc = psm.tile([P, W], F32, name="macc%d" % a, tag="macc%d" % a)
+                    maccs.append(macc)
+                for m in range(NPASS):
+                    grp = grpp.tile([P, W, 4], BF16, name="grp", tag="grp", align_bytes=64)
+                    if half == 0:
+                        x2t = wk.tile([P, 4, W], BF16, name="x2t", tag="x2t")
+                        load_pass(x2t, x2_v, m)
+                        nc.vector.tensor_copy(out=grp[:], in_=x2t[:].rearrange("p t o -> p o t"))
+                    else:
+                        mm = m % 4
+                        nc.scalar.copy(
+                            out=grp[:].rearrange("p c (e j) -> p c e j", j=2),
+                            in_=xs[m // 4][:, :, 2 * mm : 2 * mm + 2, :].rearrange("p j e c -> p c e j"),
+                        )
+                    hq = cdp.tile([P, W], U32, name="hq", tag="hq", align_bytes=64)
+                    hs = cdp.tile([P, W], U8, name="hs", tag="hs", align_bytes=64)
+                    nc.vector.quantize_mx(out=hq[:].bitcast(E4), scales=hs[:], in_=grp[:].rearrange("p o t -> p (o t)"))
+                    for a in range(4):
+                        cols = slice(P * a, P * (a + 1))
+                        nc.tensor.matmul_mx(
+                            out=maccs[a][:], lhsT=hq[:, cols].bitcast(E4), lhsT_scale=hs[:, cols],
+                            rhs=dzq[:, m, :].bitcast(E5), rhs_scale=dzs[:, m, :],
+                            start=(m == 0), stop=(m == NPASS - 1),
+                        )
+                    step = NPASS * half + m
+                    if step % 2 == 0:
+                        p_chunk(step // 2)
+                    else:
+                        small_product(step // 2)
+                for a in range(4):
+                    o1 = late.tile([P, W], F32, name="o1", tag="o1")
+                    nc.scalar.activation(out=o1[:], in_=maccs[a][:], func=ACT.Copy, scale=-1.0)
+                    r0 = 512 + 1024 * half + P * a
+                    nc.scalar.dma_start(out=out_1[r0 : r0 + P, :], in_=o1[:])

@@ -1,7 +1,7 @@
 from contextlib import ExitStack
 
 import concourse.mybir as mybir
-from concourse.masks import make_block_diagonal, make_identity
+from concourse.masks import make_identity
 
 F32 = mybir.dt.float32
 BF16 = mybir.dt.bfloat16
@@ -11,6 +11,7 @@ E4 = mybir.dt.float8_e4m3fn_x4
 E5 = mybir.dt.float8_e5m2_x4
 ACT = mybir.ActivationFunctionType
 ALU = mybir.AluOpType
+AX = mybir.AxisListType
 
 FLOPS = 2 * (2 * 4096 * 512 * 1024) + 2 * (2 * 256 * 512 * 512)
 
@@ -30,220 +31,384 @@ def tile_differentiablelogicmachine_pa_v_kernel(tc, x1, x2, W2, b2, z, grad_out,
     x1b_v = x1.rearrange("b (k j) c -> j (b k) c", j=2)
     out0_v = out_0.rearrange("b i j c -> (b i j) c")
 
-    def load_pass(tile, view, m):
-        for e in (0, 1):
-            nc.sync.dma_start(
-                out=tile[:, 2 * e : 2 * e + 2, :].rearrange("p t o -> p (t o)"), in_=view[m, e]
-            )
-
     with ExitStack() as ctx:
         const = ctx.enter_context(tc.tile_pool(name="const", bufs=1))
+        psum = ctx.enter_context(tc.psum_pool(name="psum", bufs=1))
+        grpp = ctx.enter_context(tc.tile_pool(name="grpp", bufs=2))
+        cdp = ctx.enter_context(tc.tile_pool(name="cdp", bufs=3))
+        x2p = ctx.enter_context(tc.tile_pool(name="x2p", bufs=4))
+
+        def bank(n):
+            return psum.tile([P, 4, P], F32, name="bank%d" % n, tag="bank%d" % n)
+
+        def flat(t):
+            return t[:].rearrange("p f r -> p (f r)")
+
         ident = const.tile([P, P], F32, name="ident", tag="ident")
-        bm = const.tile([P, P], F32, name="bm", tag="bm")
-        cio = const.tile([P, P], F32, name="cio", tag="cio")
-        sel_a = const.tile([P, 8, P], F32, name="sel_a", tag="sel_a")
         x1a = const.tile([P, 2, W], F32, name="x1a", tag="x1a")
         x1b = const.tile([P, 2, W], F32, name="x1b", tag="x1b")
+        x1ar = const.tile([P, 2, W], BF16, name="x1ar", tag="x1ar")
+        x1br = const.tile([P, 2, W], BF16, name="x1br", tag="x1br")
+        wraw = const.tile([P, 8, W], BF16, name="wraw", tag="wraw")
+        vgrp = const.tile([P, 4096], BF16, name="vgrp", tag="vgrp", align_bytes=64)
         vq = const.tile([P, 1024], U32, name="vq", tag="vq", align_bytes=64)
         vs = const.tile([P, 1024], U8, name="vs", tag="vs", align_bytes=64)
         dzq = const.tile([P, NPASS, W], U32, name="dzq", tag="dzq", align_bytes=64)
         dzs = const.tile([P, NPASS, W], U8, name="dzs", tag="dzs", align_bytes=64)
         nst = const.tile([P, 4096 * 4], BF16, name="nst", tag="nst", align_bytes=64)
+        dzb = const.tile([P, NPASS, 4, W], BF16, name="dzb", tag="dzb")
         p_b = const.tile([P, 2, W], F32, name="p_b", tag="p_b")
         s_a = const.tile([P, 2, W], F32, name="s_a", tag="s_a")
+        sat = const.tile([P, 4, 2, 16, 8], F32, name="sat", tag="sat")
+        sbt = const.tile([P, 2, 4, P], F32, name="sbt", tag="sbt")
         warm = const.tile([P, 1], F32, name="warm", tag="warm")
 
         nc.vector.memset(warm[:], 0.0)
         nc.scalar.activation(out=warm[:], in_=warm[:], func=ACT.Sigmoid)
-
         make_identity(nc, ident[:])
-        make_block_diagonal(nc, bm[:], 8)
-        nc.gpsimd.iota(
-            cio[:], pattern=[[0, 16], [1, 8]], base=0, channel_multiplier=0, allow_small_or_imprecise_dtypes=True
-        )
-        for v in range(8):
-            nc.vector.scalar_tensor_tensor(
-                out=sel_a[:, v, :], in0=cio[:], scalar=float(v), in1=bm[:], op0=ALU.is_equal, op1=ALU.mult
-            )
 
         nw = nst[:].bitcast(F32)
         n_v = nw.rearrange("p (b m e k x) -> p m e b k x", b=16, m=NPASS, e=2, k=8, x=4)
+        dzw = dzb[:].bitcast(F32)
 
-        with tc.tile_pool(name="vprep", bufs=1) as vp, tc.psum_pool(name="psv", bufs=2) as psv:
-            wraw = vp.tile([P, 8, W], BF16, name="wraw", tag="wraw")
-            for s in (0, 1):
+        ctx.enter_context(tc.manual_schedule())
+
+        x2ts = {}
+
+        def load_x2(n):
+            x2t = x2p.tile([P, 4, W], BF16, name="x2t", tag="x2t")
+            if n < 8:
+                for e in (0, 1):
+                    nc.sync.dma_start(
+                        out=x2t[:, 2 * e : 2 * e + 2, :].rearrange("p t o -> p (t o)"), in_=x2_v[n, e]
+                    )
+            else:
+                i0 = 2 * (n - 8)
                 nc.sync.dma_start(
-                    out=wraw[:, 4 * s : 4 * s + 4, :],
-                    in_=W2[512 + 1024 * s : 1024 + 1024 * s, :].rearrange("(r p) o -> p r o", p=P),
+                    out=x2t[:].rearrange("p (j e) c -> p j e c", e=2), in_=x2s_v[:, :, i0 : i0 + 2, :]
                 )
-            x1ar = vp.tile([P, 2, W], BF16, name="x1ar", tag="x1ar")
-            x1br = vp.tile([P, 2, W], BF16, name="x1br", tag="x1br")
-            for q in (0, 1):
-                nc.sync.dma_start(out=x1ar[:, q, :], in_=x1a_v[q])
-                nc.sync.dma_start(out=x1br[:, q, :], in_=x1b_v[q])
-            nc.vector.tensor_copy(out=x1a[:], in_=x1ar[:])
-            nc.vector.tensor_copy(out=x1b[:], in_=x1br[:])
+            x2ts[n] = x2t
 
-            vgrp = vp.tile([P, 4096], BF16, name="vgrp", tag="vgrp", align_bytes=64)
-            vgw = vgrp[:].bitcast(F32)
-            for a2 in range(4):
-                vps = psv.tile([P, 2, 2, P], F32, name="vps", tag="vps")
-                for a in (0, 1):
-                    words = wraw[:, 2 * a2 + a, :].bitcast(F32)
-                    for u in (0, 1):
-                        nc.tensor.transpose(vps[:, a, u, :], words[:, u:256:2], ident[:])
-                nc.vector.tensor_copy(
-                    out=vgw[:, 512 * a2 : 512 * (a2 + 1)].rearrange("p (a r u) -> p a r u", a=2, u=2),
-                    in_=vps[:].rearrange("p a u r -> p a r u"),
+        def back_t(src, n):
+            bk = bank(n)
+            for fc in range(4):
+                nc.tensor.transpose(bk[:, fc, :], src[fc], ident[:])
+            return bk
+
+        acc_b = [bank(5), bank(6)]
+        zts = {}
+        gts = {}
+        tpss = {}
+        accas = {}
+        grps = {}
+        hqs = {}
+
+        def x2i(s):
+            grp = grpp.tile([P, W, 4], BF16, name="grph", tag="grph", bufs=3, align_bytes=64)
+            nc.scalar.copy(out=grp[:], in_=x2ts[s][:].rearrange("p t o -> p o t"))
+            grps[s] = grp
+
+        def dzi_qh_qd(s):
+            grd = grpp.tile([P, W, 4], BF16, name="grpd", tag="grpd", align_bytes=64)
+            nc.vector.tensor_copy(out=grd[:], in_=dzb[:, s, :, :].rearrange("p t o -> p o t"))
+            q_h(s)
+            nc.vector.quantize_mx(
+                out=dzq[:, s, :].bitcast(E5), scales=dzs[:, s, :], in_=grd[:].rearrange("p o t -> p (o t)")
+            )
+
+        def q_h(s):
+            hq = cdp.tile([P, W], U32, name="hq", tag="hq", align_bytes=64)
+            hs = cdp.tile([P, W], U8, name="hs", tag="hs", align_bytes=64)
+            nc.vector.quantize_mx(
+                out=hq[:].bitcast(E4), scales=hs[:], in_=grps[s][:].rearrange("p o t -> p (o t)")
+            )
+            hqs[s] = (hq, hs)
+
+        with tc.tile_pool(name="zp", bufs=4) as zp:
+
+            def load_zg(m):
+                zt = zp.tile([P, 4, W], F32, name="zt", tag="zt")
+                gt = zp.tile([P, 4, W], BF16, name="gt", tag="gt")
+                for e in (0, 1):
+                    sl = slice(2 * e, 2 * e + 2)
+                    nc.sync.dma_start(out=zt[:, sl, :].rearrange("p t o -> p (t o)"), in_=z_v[m, e])
+                    nc.sync.dma_start(out=gt[:, sl, :].rearrange("p t o -> p (t o)"), in_=g_v[m, e])
+                zts[m] = zt
+                gts[m] = gt
+
+            def half(t, h):
+                return t[h // 2][:, 2 * (h % 2) : 2 * (h % 2) + 2, :]
+
+            def s12(h):
+                ze = half(zts, h)
+                nc.scalar.activation(out=ze, in_=ze, func=ACT.Sigmoid)
+                nc.scalar.activation(out=ze, in_=ze, func=ACT.Square, bias=-0.5)
+
+            def v1(h):
+                ze = half(zts, h)
+                nc.vector.scalar_tensor_tensor(
+                    out=ze, in0=ze, scalar=0.25, in1=half(gts, h), op0=ALU.subtract, op1=ALU.mult
                 )
-            nc.vector.quantize_mx(out=vq[:].bitcast(E4), scales=vs[:], in_=vgrp[:])
+
+            def cast(h):
+                nc.vector.tensor_copy(out=dzb[:, h // 2, 2 * (h % 2) : 2 * (h % 2) + 2, :], in_=half(zts, h))
+
+            def pe1(h):
+                m = h // 2
+                e = h % 2
+                tps = bank(h % 3)
+                for jl in (0, 1):
+                    for u in (0, 1):
+                        nc.tensor.transpose(tps[:, 2 * jl + u, :], dzw[:, m, 2 * e + jl, u:256:2], ident[:])
+                tpss[h] = tps
+                acc_a = bank(3 + e)
+                for jl in (0, 1):
+                    for fc in range(4):
+                        blk = zts[m][:, 2 * e + jl, P * fc : P * (fc + 1)]
+                        nc.tensor.matmul(
+                            out=acc_a[:, fc, :], lhsT=blk, rhs=ident[:], is_transpose=True,
+                            start=(jl == 0 and fc == 0), stop=(jl == 1 and fc == 3),
+                        )
+                        nc.tensor.matmul(
+                            out=acc_b[jl][:, fc, :], lhsT=blk, rhs=ident[:], is_transpose=True,
+                            start=(h == 0 and fc == 0), stop=(h == 15 and fc == 3),
+                        )
+                accas[h] = acc_a
+
+            def evac_n(h):
+                dst = n_v[:, h // 2, h % 2]
+                src = tpss[h][:].rearrange("p x (b k) -> p b k x", k=8)
+                if h % 2 == 0:
+                    nc.scalar.copy(out=dst, in_=src)
+                else:
+                    nc.vector.tensor_copy(out=dst, in_=src)
+
+            def red(h):
+                m = h // 2
+                nc.vector.tensor_reduce(
+                    out=sat[:, :, m // 4, :, 2 * (m % 4) + h % 2],
+                    in_=accas[h][:].rearrange("p f (b k) -> p f b k", k=8),
+                    axis=AX.X, op=ALU.add,
+                )
+
+            for m in range(4):
+                load_zg(m)
+            bk_a0 = None
+            for it in range(19):
+                if it < 16:
+                    s12(it)
+                if it == 16:
+                    x2i(0)
+                if 3 <= it and (it - 3) % 2 == 0:
+                    evac_n(it - 3)
+                if it == 12:
+                    nc.scalar.copy(out=s_a[:, 0, :], in_=flat(bk_a0))
+                if it == 17:
+                    x2i(1)
+                if 1 <= it <= 16:
+                    v1(it - 1)
+                if 3 <= it:
+                    red(it - 3)
+                if 1 <= it <= 16:
+                    cast(it - 1)
+                if 3 <= it and (it - 3) % 2 == 1:
+                    evac_n(it - 3)
+                if it == 17:
+                    dzi_qh_qd(0)
+                if 2 <= it <= 17:
+                    pe1(it - 2)
+                if it == 11:
+                    bk_a0 = back_t([sat[:, fc, 0, :, :].rearrange("p b v -> p (b v)") for fc in range(4)], 7)
+                if it % 2 == 1 and 3 <= it <= 9:
+                    load_zg((it - 3) // 2 + 4)
+                if it == 9:
+                    for q in (0, 1):
+                        nc.sync.dma_start(out=x1ar[:, q, :], in_=x1a_v[q])
+                        nc.sync.dma_start(out=x1br[:, q, :], in_=x1b_v[q])
+                    for n in range(4):
+                        load_x2(n)
+                    for s in (0, 1):
+                        nc.sync.dma_start(
+                            out=wraw[:, 4 * s : 4 * s + 4, :],
+                            in_=W2[512 + 1024 * s : 1024 + 1024 * s, :].rearrange("(r p) o -> p r o", p=P),
+                        )
 
         late = ctx.enter_context(tc.tile_pool(name="late", bufs=2))
         ostp = ctx.enter_context(tc.tile_pool(name="ostp", bufs=4))
-        zp = ctx.enter_context(tc.tile_pool(name="zp", bufs=3))
-        wk = ctx.enter_context(tc.tile_pool(name="wk", bufs=2))
-        grpp = ctx.enter_context(tc.tile_pool(name="grpp", bufs=3))
-        cdp = ctx.enter_context(tc.tile_pool(name="cdp", bufs=3))
+        nqa = late.tile([P, 8, W], U32, name="nqa", tag="nqa", bufs=1, align_bytes=64)
+        nqsa = late.tile([P, 8, W], U8, name="nqsa", tag="nqsa", bufs=1, align_bytes=64)
+        ssts = {}
+        sqs = {}
+        dds = {}
+        vpss = {}
+        paccs = {}
+        m_banks = (7, 1, 3, 2)
+        p_banks = (4, 5, 6, 0)
 
-        with tc.psum_pool(name="ps1", bufs=2) as ps1:
-            sa_ps = None
-            for m in range(NPASS):
-                zt = zp.tile([P, 4, W], F32, name="zt", tag="zt")
-                gt = zp.tile([P, 4, W], BF16, name="gt", tag="gt")
-                load_pass(zt, z_v, m)
-                load_pass(gt, g_v, m)
-                dzb = wk.tile([P, 4, W], BF16, name="dzb", tag="dzb")
-                pa = wk.tile([P, 2, W], F32, name="pa", tag="pa")
-                for e in (0, 1):
-                    ze = zt[:, 2 * e : 2 * e + 2, :]
-                    nc.scalar.activation(out=ze, in_=ze, func=ACT.Sigmoid)
-                    nc.scalar.activation(out=ze, in_=ze, func=ACT.Square, bias=-0.5)
-                    nc.vector.scalar_tensor_tensor(
-                        out=ze, in0=ze, scalar=0.25, in1=gt[:, 2 * e : 2 * e + 2, :], op0=ALU.subtract, op1=ALU.mult
-                    )
-                    nc.scalar.copy(out=dzb[:, 2 * e : 2 * e + 2, :], in_=ze)
-                    nc.vector.tensor_tensor(
-                        out=pa[:, e, :], in0=zt[:, 2 * e, :], in1=zt[:, 2 * e + 1, :], op=ALU.add
-                    )
-                if m == 0:
-                    nc.vector.tensor_tensor(out=p_b[:], in0=zt[:, 0:2, :], in1=zt[:, 2:4, :], op=ALU.add)
-                else:
-                    tb = wk.tile([P, 2, W], F32, name="tb", tag="tb")
-                    nc.vector.tensor_tensor(out=tb[:], in0=zt[:, 0:2, :], in1=zt[:, 2:4, :], op=ALU.add)
-                    nc.vector.tensor_tensor(out=p_b[:], in0=p_b[:], in1=tb[:], op=ALU.add)
+        def negate_out(eng, out, in_):
+            if eng == 0:
+                nc.scalar.activation(out=out, in_=in_, func=ACT.Copy, scale=-1.0)
+            else:
+                nc.vector.tensor_scalar(out=out, in0=in_, scalar1=-1.0, scalar2=None, op0=ALU.mult)
 
-                grp = grpp.tile([P, W, 4], BF16, name="grp", tag="grp", align_bytes=64)
-                nc.vector.tensor_copy(out=grp[:], in_=dzb[:].rearrange("p t o -> p o t"))
-                nc.vector.quantize_mx(
-                    out=dzq[:, m, :].bitcast(E5), scales=dzs[:, m, :], in_=grp[:].rearrange("p o t -> p (o t)")
+        def qn(c):
+            nc.vector.quantize_mx(
+                out=nqa[:, c, :].bitcast(E5), scales=nqsa[:, c, :], in_=nst[:, 2048 * c : 2048 * (c + 1)]
+            )
+
+        def x2si(c):
+            grp = grpp.tile([P, W, 4], BF16, name="grph", tag="grph", bufs=3, align_bytes=64)
+            nc.vector.tensor_copy(
+                out=grp[:].rearrange("p c (e j) -> p c e j", j=2),
+                in_=x2ts[8 + c][:].rearrange("p (j e) c -> p c e j", e=2),
+            )
+            grps[8 + c] = grp
+
+        def scp(c, sc):
+            if sc == 1:
+                sst = late.tile([P, 2048], BF16, name="sst", tag="sst", align_bytes=64)
+                ssts[c] = sst
+            b = 2 * c + sc
+            dst = ssts[c][:, 1024 * sc : 1024 * (sc + 1)].rearrange("p (i j t) -> p i j t", i=16, j=16)
+            src = nst[:, 1024 * b : 1024 * (b + 1)].rearrange("p (j i t) -> p i j t", i=16, j=16)
+            if sc == 0:
+                nc.vector.tensor_copy(out=dst, in_=src)
+            else:
+                nc.scalar.copy(out=dst, in_=src)
+
+        def qs(c):
+            sq = cdp.tile([P, W], U32, name="sq", tag="sq", align_bytes=64)
+            sqsc = cdp.tile([P, W], U8, name="sqsc", tag="sqsc", align_bytes=64)
+            nc.vector.quantize_mx(out=sq[:].bitcast(E5), scales=sqsc[:], in_=ssts[c][:])
+            sqs[c] = (sq, sqsc)
+
+        def m_step(maccs, s):
+            hq, hs = hqs[s]
+            m = s % 8
+            for a in range(4):
+                cols = slice(P * a, P * (a + 1))
+                nc.tensor.matmul_mx(
+                    out=flat(maccs[a]), lhsT=hq[:, cols].bitcast(E4), lhsT_scale=hs[:, cols],
+                    rhs=dzq[:, m, :].bitcast(E5), rhs_scale=dzs[:, m, :],
+                    start=(m == 0), stop=(m == NPASS - 1),
                 )
 
-                dzw = dzb[:].bitcast(F32)
-                for e in (0, 1):
-                    tps = ps1.tile([P, 4, P], F32, name="tps", tag="tps", bufs=3)
-                    for jl in (0, 1):
-                        for u in (0, 1):
-                            nc.tensor.transpose(tps[:, 2 * jl + u, :], dzw[:, 2 * e + jl, u:256:2], ident[:])
-                    nc.scalar.copy(out=n_v[:, m, e], in_=tps[:].rearrange("p x (b k) -> p b k x", k=8))
+        def m_evac(maccs, sweep, a):
+            o1 = late.tile([P, W], F32, name="o1", tag="o1", bufs=6)
+            negate_out(a % 2, o1[:], flat(maccs[a]))
+            r0 = 512 + 1024 * sweep + P * a
+            nc.sync.dma_start(out=out_1[r0 : r0 + P, :], in_=o1[:])
 
-                if m % 4 == 0:
-                    sa_ps = ps1.tile([P, W], F32, name="sa_ps", tag="sa_ps", bufs=2)
-                for e in (0, 1):
-                    v = 2 * (m % 4) + e
-                    nc.tensor.matmul(
-                        out=sa_ps[:], lhsT=sel_a[:, v, :], rhs=pa[:, e, :], start=(v == 0), stop=(v == 7)
-                    )
-                if m % 4 == 3:
-                    nc.vector.tensor_copy(out=s_a[:, m // 4, :], in_=sa_ps[:])
+        def dd(n):
+            cc = n % 4
+            acc = bank(6 if n % 2 == 0 else 0)
+            lhs = x1a if n < 4 else x1b
+            rhs = s_a if n < 4 else p_b
+            for q in (0, 1):
+                nc.tensor.matmul(
+                    out=flat(acc), lhsT=lhs[:, q, P * cc : P * (cc + 1)], rhs=rhs[:, q, :], start=(q == 0), stop=(q == 1)
+                )
+            dds[n] = acc
 
-        with tc.psum_pool(name="ps2", bufs=2) as ps2, tc.psum_pool(name="psm", bufs=1) as psm:
-            xs = []
-            for hm in (0, 1):
-                xst = late.tile([P, 2, 8, W], BF16, name="xst", tag="xst")
-                nc.sync.dma_start(out=xst[:], in_=x2s_v[:, :, 8 * hm : 8 * hm + 8, :])
-                xs.append(xst)
+        def dd_evac(n):
+            o1 = late.tile([P, W], F32, name="o1", tag="o1", bufs=6)
+            negate_out(0, o1[:], flat(dds[n]))
+            r0 = P * (n % 4) + (0 if n < 4 else 1024)
+            nc.sync.dma_start(out=out_1[r0 : r0 + P, :], in_=o1[:])
 
-            def small_product(n):
-                cc = n % 4
-                acc = ps2.tile([P, W], F32, name="dd", tag="dd")
-                for q in (0, 1):
-                    if n < 4:
-                        nc.tensor.matmul(
-                            out=acc[:], lhsT=x1a[:, q, P * cc : P * (cc + 1)], rhs=s_a[:, q, :], start=(q == 0), stop=(q == 1)
-                        )
-                    else:
-                        nc.tensor.matmul(
-                            out=acc[:], lhsT=x1b[:, q, P * cc : P * (cc + 1)], rhs=p_b[:, q, :], start=(q == 0), stop=(q == 1)
-                        )
-                o1 = late.tile([P, W], F32, name="o1", tag="o1")
-                nc.scalar.activation(out=o1[:], in_=acc[:], func=ACT.Copy, scale=-1.0)
-                r0 = P * cc + (0 if n < 4 else 1024)
-                nc.scalar.dma_start(out=out_1[r0 : r0 + P, :], in_=o1[:])
+        def vprep_t(a2):
+            vps = bank(4 + a2 % 2)
+            for a in (0, 1):
+                words = wraw[:, 2 * a2 + a, :].bitcast(F32)
+                for u in (0, 1):
+                    nc.tensor.transpose(vps[:, 2 * a + u, :], words[:, u:256:2], ident[:])
+            vpss[a2] = vps
 
-            def p_chunk(c):
-                nq = cdp.tile([P, W], U32, name="nq", tag="nq", bufs=2, align_bytes=64)
-                nqs = cdp.tile([P, W], U8, name="nqs", tag="nqs", bufs=2, align_bytes=64)
-                nc.vector.quantize_mx(out=nq[:].bitcast(E5), scales=nqs[:], in_=nst[:, 2048 * c : 2048 * (c + 1)])
-                sst = late.tile([P, 2048], BF16, name="sst", tag="sst", align_bytes=64)
-                for sc in (0, 1):
-                    b = 2 * c + sc
-                    nc.vector.tensor_copy(
-                        out=sst[:, 1024 * sc : 1024 * (sc + 1)].rearrange("p (i j t) -> p i j t", i=16, j=16),
-                        in_=nst[:, 1024 * b : 1024 * (b + 1)].rearrange("p (j i t) -> p i j t", i=16, j=16),
-                    )
-                sq = cdp.tile([P, W], U32, name="sq", tag="sq", bufs=2, align_bytes=64)
-                sqs = cdp.tile([P, W], U8, name="sqs", tag="sqs", bufs=2, align_bytes=64)
-                nc.vector.quantize_mx(out=sq[:].bitcast(E5), scales=sqs[:], in_=sst[:])
+        def vprep_e(a2):
+            nc.vector.tensor_copy(
+                out=vgrp[:].bitcast(F32)[:, 512 * a2 : 512 * (a2 + 1)].rearrange("p (a r u) -> p a r u", a=2, u=2),
+                in_=vpss[a2][:].rearrange("p (a u) r -> p a r u", u=2),
+            )
+
+        def p_mm(c):
+            sq, sqsc = sqs[c]
+            for a in range(4):
+                cols = slice(P * a, P * (a + 1))
+                acc = bank(p_banks[a])
+                nc.tensor.matmul_mx(
+                    out=flat(acc), lhsT=nqa[:, c, cols].bitcast(E5), lhsT_scale=nqsa[:, c, cols],
+                    rhs=vq[:, 0:512].bitcast(E4), rhs_scale=vs[:, 0:512], start=True, stop=False,
+                )
+                nc.tensor.matmul_mx(
+                    out=flat(acc), lhsT=sq[:, cols].bitcast(E5), lhsT_scale=sqsc[:, cols],
+                    rhs=vq[:, 512:1024].bitcast(E4), rhs_scale=vs[:, 512:1024], start=False, stop=True,
+                )
+                paccs[(c, a)] = acc
+
+        def p_evac(c, a):
+            ost = ostp.tile([P, W], F32, name="ost", tag="ost")
+            negate_out(a % 2 if c == 7 else 0, ost[:], flat(paccs[(c, a)]))
+            r0 = 512 * c + P * a
+            nc.sync.dma_start(out=out0_v[r0 : r0 + P, :], in_=ost[:])
+
+        load_x2(4)
+        load_x2(5)
+        nc.vector.tensor_copy(out=x1a[:], in_=x1ar[:])
+        nc.vector.tensor_copy(out=x1b[:], in_=x1br[:])
+        for jl in (0, 1):
+            nc.scalar.copy(out=sbt[:, jl, :, :], in_=acc_b[jl][:])
+        maccs = [bank(n) for n in m_banks]
+        m_step(maccs, 0)
+        bk_b0 = back_t([sbt[:, 0, fc, :] for fc in range(4)], 4)
+        bk_b1 = back_t([sbt[:, 1, fc, :] for fc in range(4)], 5)
+        bk_a1 = back_t([sat[:, fc, 1, :, :].rearrange("p b v -> p (b v)") for fc in range(4)], 0)
+        nc.scalar.copy(out=s_a[:, 1, :], in_=flat(bk_a1))
+        nc.scalar.copy(out=p_b[:, 0, :], in_=flat(bk_b0))
+        nc.scalar.copy(out=p_b[:, 1, :], in_=flat(bk_b1))
+
+        for s in range(16):
+            if s + 2 < 8:
+                x2i(s + 2)
+                load_x2(s + 6)
+            if 1 <= s <= 8:
+                dd_evac(s - 1)
+            if 7 <= s <= 14:
+                scp(s - 7, 1)
+            if s + 1 < 8:
+                dzi_qh_qd(s + 1)
+            if s < 8:
+                qn(s)
+            if 2 <= s <= 5:
+                vprep_e(s - 2)
+            if s == 6:
+                nc.vector.quantize_mx(out=vq[:].bitcast(E4), scales=vs[:], in_=vgrp[:])
+            if s == 7:
                 for a in range(4):
-                    cols = slice(P * a, P * (a + 1))
-                    acc = ps2.tile([P, W], F32, name="pp", tag="pp")
-                    nc.tensor.matmul_mx(
-                        out=acc[:], lhsT=nq[:, cols].bitcast(E5), lhsT_scale=nqs[:, cols],
-                        rhs=vq[:, 0:512].bitcast(E4), rhs_scale=vs[:, 0:512], start=True, stop=False,
-                    )
-                    nc.tensor.matmul_mx(
-                        out=acc[:], lhsT=sq[:, cols].bitcast(E5), lhsT_scale=sqs[:, cols],
-                        rhs=vq[:, 512:1024].bitcast(E4), rhs_scale=vs[:, 512:1024], start=False, stop=True,
-                    )
-                    ost = ostp.tile([P, W], F32, name="ost", tag="ost")
-                    nc.scalar.activation(out=ost[:], in_=acc[:], func=ACT.Copy, scale=-1.0)
-                    r0 = 512 * c + P * a
-                    nc.scalar.dma_start(out=out0_v[r0 : r0 + P, :], in_=ost[:])
-
-            for half in (0, 1):
-                maccs = []
-                for a in range(4):
-                    macc = psm.tile([P, W], F32, name="macc%d" % a, tag="macc%d" % a)
-                    maccs.append(macc)
-                for m in range(NPASS):
-                    grp = grpp.tile([P, W, 4], BF16, name="grp", tag="grp", align_bytes=64)
-                    if half == 0:
-                        x2t = wk.tile([P, 4, W], BF16, name="x2t", tag="x2t")
-                        load_pass(x2t, x2_v, m)
-                        nc.vector.tensor_copy(out=grp[:], in_=x2t[:].rearrange("p t o -> p o t"))
-                    else:
-                        mm = m % 4
-                        nc.scalar.copy(
-                            out=grp[:].rearrange("p c (e j) -> p c e j", j=2),
-                            in_=xs[m // 4][:, :, 2 * mm : 2 * mm + 2, :].rearrange("p j e c -> p c e j"),
-                        )
-                    hq = cdp.tile([P, W], U32, name="hq", tag="hq", align_bytes=64)
-                    hs = cdp.tile([P, W], U8, name="hs", tag="hs", align_bytes=64)
-                    nc.vector.quantize_mx(out=hq[:].bitcast(E4), scales=hs[:], in_=grp[:].rearrange("p o t -> p (o t)"))
+                    m_evac(maccs, 0, a)
+            if 7 <= s <= 14:
+                c = s - 7
+                x2si(c)
+                if c + 12 < 16:
+                    load_x2(c + 12)
+                scp(c, 0)
+                q_h(8 + c)
+                qs(c)
+            if s < 8:
+                dd(s)
+                if s + 1 < 8:
+                    m_step(maccs, s + 1)
+                if 1 <= s <= 4:
+                    vprep_t(s - 1)
+            else:
+                if s == 8:
+                    maccs = [bank(n) for n in m_banks]
+                if s < 15:
+                    p_mm(s - 8)
+                    m_step(maccs, s)
+                else:
+                    m_step(maccs, s)
+                    p_mm(s - 8)
                     for a in range(4):
-                        cols = slice(P * a, P * (a + 1))
-                        nc.tensor.matmul_mx(
-                            out=maccs[a][:], lhsT=hq[:, cols].bitcast(E4), lhsT_scale=hs[:, cols],
-                            rhs=dzq[:, m, :].bitcast(E5), rhs_scale=dzs[:, m, :],
-                            start=(m == 0), stop=(m == NPASS - 1),
-                        )
-                    step = NPASS * half + m
-                    if step % 2 == 0:
-                        p_chunk(step // 2)
-                    else:
-                        small_product(step // 2)
+                        m_evac(maccs, 1, a)
                 for a in range(4):
-                    o1 = late.tile([P, W], F32, name="o1", tag="o1")
-                    nc.scalar.activation(out=o1[:], in_=maccs[a][:], func=ACT.Copy, scale=-1.0)
-                    r0 = 512 + 1024 * half + P * a
-                    nc.scalar.dma_start(out=out_1[r0 : r0 + P, :], in_=o1[:])
+                    p_evac(s - 8, a)

@@ -7,6 +7,7 @@ F32 = mybir.dt.float32
 BF16 = mybir.dt.bfloat16
 U32 = mybir.dt.uint32
 U8 = mybir.dt.uint8
+I32 = mybir.dt.int32
 E4 = mybir.dt.float8_e4m3fn_x4
 E5 = mybir.dt.float8_e5m2_x4
 ACT = mybir.ActivationFunctionType
@@ -27,9 +28,9 @@ def tile_differentiablelogicmachine_pa_v_kernel(tc, x1, x2, W2, b2, z, grad_out,
     g_v = grad_out.rearrange("b (m e) (k j) o -> m e b k (j o)", e=2, j=2)
     x2_v = x2.rearrange("b (m e) (k j) o -> m e b k (j o)", e=2, j=2)
     x2s_v = x2.rearrange("b (k j) i c -> (b k) j i c", j=2)
-    x1a_v = x1.rearrange("b (q v) c -> q b v c", v=8)
+    x1a_v = x1.rearrange("b (q v) c -> q v b c", v=8)
     x1b_v = x1.rearrange("b (k j) c -> j (b k) c", j=2)
-    out0_v = out_0.rearrange("b i j c -> (b i j) c")
+    out0_v = out_0.rearrange("b i (h j) c -> i h j b c", j=8)
 
     with ExitStack() as ctx:
         const = ctx.enter_context(tc.tile_pool(name="const", bufs=1))
@@ -59,7 +60,7 @@ def tile_differentiablelogicmachine_pa_v_kernel(tc, x1, x2, W2, b2, z, grad_out,
         dzb = const.tile([P, NPASS, 4, W], BF16, name="dzb", tag="dzb")
         p_b = const.tile([P, 2, W], F32, name="p_b", tag="p_b")
         s_a = const.tile([P, 2, W], F32, name="s_a", tag="s_a")
-        sat = const.tile([P, 4, 2, 16, 8], F32, name="sat", tag="sat")
+        sat = const.tile([P, 4, 16, 16], F32, name="sat", tag="sat")
         sbt = const.tile([P, 2, 4, P], F32, name="sbt", tag="sbt")
         warm = const.tile([P, 1], F32, name="warm", tag="warm")
 
@@ -68,7 +69,7 @@ def tile_differentiablelogicmachine_pa_v_kernel(tc, x1, x2, W2, b2, z, grad_out,
         make_identity(nc, ident[:])
 
         nw = nst[:].bitcast(F32)
-        n_v = nw.rearrange("p (b m e k x) -> p m e b k x", b=16, m=NPASS, e=2, k=8, x=4)
+        n_v = nw.rearrange("p (i k j b u) -> p i j k b u", i=16, k=8, j=2, b=16, u=2)
         dzw = dzb[:].bitcast(F32)
 
         ctx.enter_context(tc.manual_schedule())
@@ -176,17 +177,17 @@ def tile_differentiablelogicmachine_pa_v_kernel(tc, x1, x2, W2, b2, z, grad_out,
                 accas[h] = acc_a
 
             def evac_n(h):
-                dst = n_v[:, h // 2, h % 2]
-                src = tpss[h][:].rearrange("p x (b k) -> p b k x", k=8)
-                if h % 2 == 0:
-                    nc.scalar.copy(out=dst, in_=src)
-                else:
-                    nc.vector.tensor_copy(out=dst, in_=src)
+                for jl in (0, 1):
+                    dst = n_v[:, h, jl]
+                    src = tpss[h][:, 2 * jl : 2 * jl + 2, :].rearrange("p u (b k) -> p k b u", k=8)
+                    if h % 2 == 0:
+                        nc.scalar.copy(out=dst, in_=src)
+                    else:
+                        nc.vector.tensor_copy(out=dst, in_=src)
 
             def red(h):
-                m = h // 2
                 nc.vector.tensor_reduce(
-                    out=sat[:, :, m // 4, :, 2 * (m % 4) + h % 2],
+                    out=sat[:, :, h, :],
                     in_=accas[h][:].rearrange("p f (b k) -> p f b k", k=8),
                     axis=AX.X, op=ALU.add,
                 )
@@ -194,6 +195,11 @@ def tile_differentiablelogicmachine_pa_v_kernel(tc, x1, x2, W2, b2, z, grad_out,
             for m in range(4):
                 load_zg(m)
             bk_a0 = None
+            heat = bank(7)
+            for n in range(7):
+                nc.tensor.matmul(
+                    out=flat(heat), lhsT=gts[0][:, 0, 0:P], rhs=gts[0][:, 0, :], start=True, stop=True
+                )
             for it in range(19):
                 if it < 16:
                     s12(it)
@@ -218,7 +224,7 @@ def tile_differentiablelogicmachine_pa_v_kernel(tc, x1, x2, W2, b2, z, grad_out,
                 if 2 <= it <= 17:
                     pe1(it - 2)
                 if it == 11:
-                    bk_a0 = back_t([sat[:, fc, 0, :, :].rearrange("p b v -> p (b v)") for fc in range(4)], 7)
+                    bk_a0 = back_t([sat[:, fc, 0:8, :].rearrange("p v b -> p (v b)") for fc in range(4)], 7)
                 if it % 2 == 1 and 3 <= it <= 9:
                     load_zg((it - 3) // 2 + 4)
                 if it == 9:
@@ -237,7 +243,9 @@ def tile_differentiablelogicmachine_pa_v_kernel(tc, x1, x2, W2, b2, z, grad_out,
         ostp = ctx.enter_context(tc.tile_pool(name="ostp", bufs=4))
         nqa = late.tile([P, 8, W], U32, name="nqa", tag="nqa", bufs=1, align_bytes=64)
         nqsa = late.tile([P, 8, W], U8, name="nqsa", tag="nqsa", bufs=1, align_bytes=64)
-        ssts = {}
+        nc.vector.memset(nqsa[:].rearrange("p c w -> p (c w)").bitcast(I32), 0)
+        n_codes = nqa[:].rearrange("p c w -> p (c w)").bitcast(I32).rearrange("p (x y b) -> p y x b", x=16, y=16)
+        n_scales = nqsa[:].rearrange("p c w -> p (c w)").bitcast(I32).rearrange("p (x y b) -> p y x b", x=16, y=16)
         sqs = {}
         dds = {}
         vpss = {}
@@ -264,22 +272,17 @@ def tile_differentiablelogicmachine_pa_v_kernel(tc, x1, x2, W2, b2, z, grad_out,
             )
             grps[8 + c] = grp
 
-        def scp(c, sc):
-            if sc == 1:
-                sst = late.tile([P, 2048], BF16, name="sst", tag="sst", align_bytes=64)
-                ssts[c] = sst
-            b = 2 * c + sc
-            dst = ssts[c][:, 1024 * sc : 1024 * (sc + 1)].rearrange("p (i j t) -> p i j t", i=16, j=16)
-            src = nst[:, 1024 * b : 1024 * (b + 1)].rearrange("p (j i t) -> p i j t", i=16, j=16)
-            if sc == 0:
-                nc.vector.tensor_copy(out=dst, in_=src)
-            else:
-                nc.scalar.copy(out=dst, in_=src)
-
-        def qs(c):
+        def s_codes(c):
             sq = cdp.tile([P, W], U32, name="sq", tag="sq", align_bytes=64)
             sqsc = cdp.tile([P, W], U8, name="sqsc", tag="sqsc", align_bytes=64)
-            nc.vector.quantize_mx(out=sq[:].bitcast(E5), scales=sqsc[:], in_=ssts[c][:])
+            nc.vector.tensor_copy(
+                out=sq[:].bitcast(I32).rearrange("p (y x b) -> p y x b", y=2, x=16),
+                in_=n_codes[:, 2 * c : 2 * c + 2],
+            )
+            nc.vector.tensor_copy(
+                out=sqsc[:].bitcast(I32).rearrange("p (y x b) -> p y x b", y=2, x=16),
+                in_=n_scales[:, 2 * c : 2 * c + 2],
+            )
             sqs[c] = (sq, sqsc)
 
         def m_step(maccs, s):
@@ -294,7 +297,7 @@ def tile_differentiablelogicmachine_pa_v_kernel(tc, x1, x2, W2, b2, z, grad_out,
                 )
 
         def m_evac(maccs, sweep, a):
-            o1 = late.tile([P, W], F32, name="o1", tag="o1", bufs=6)
+            o1 = late.tile([P, W], F32, name="o1", tag="o1", bufs=3)
             negate_out(a % 2, o1[:], flat(maccs[a]))
             r0 = 512 + 1024 * sweep + P * a
             nc.sync.dma_start(out=out_1[r0 : r0 + P, :], in_=o1[:])
@@ -311,7 +314,7 @@ def tile_differentiablelogicmachine_pa_v_kernel(tc, x1, x2, W2, b2, z, grad_out,
             dds[n] = acc
 
         def dd_evac(n):
-            o1 = late.tile([P, W], F32, name="o1", tag="o1", bufs=6)
+            o1 = late.tile([P, W], F32, name="o1", tag="o1", bufs=3)
             negate_out(0, o1[:], flat(dds[n]))
             r0 = P * (n % 4) + (0 if n < 4 else 1024)
             nc.sync.dma_start(out=out_1[r0 : r0 + P, :], in_=o1[:])
@@ -348,8 +351,7 @@ def tile_differentiablelogicmachine_pa_v_kernel(tc, x1, x2, W2, b2, z, grad_out,
         def p_evac(c, a):
             ost = ostp.tile([P, W], F32, name="ost", tag="ost")
             negate_out(a % 2 if c == 7 else 0, ost[:], flat(paccs[(c, a)]))
-            r0 = 512 * c + P * a
-            nc.sync.dma_start(out=out0_v[r0 : r0 + P, :], in_=ost[:])
+            nc.sync.dma_start(out=out0_v[2 * c + a // 2, a % 2], in_=ost[:])
 
         load_x2(4)
         load_x2(5)
@@ -361,7 +363,7 @@ def tile_differentiablelogicmachine_pa_v_kernel(tc, x1, x2, W2, b2, z, grad_out,
         m_step(maccs, 0)
         bk_b0 = back_t([sbt[:, 0, fc, :] for fc in range(4)], 4)
         bk_b1 = back_t([sbt[:, 1, fc, :] for fc in range(4)], 5)
-        bk_a1 = back_t([sat[:, fc, 1, :, :].rearrange("p b v -> p (b v)") for fc in range(4)], 0)
+        bk_a1 = back_t([sat[:, fc, 8:16, :].rearrange("p v b -> p (v b)") for fc in range(4)], 0)
         nc.scalar.copy(out=s_a[:, 1, :], in_=flat(bk_a1))
         nc.scalar.copy(out=p_b[:, 0, :], in_=flat(bk_b0))
         nc.scalar.copy(out=p_b[:, 1, :], in_=flat(bk_b1))
@@ -372,8 +374,6 @@ def tile_differentiablelogicmachine_pa_v_kernel(tc, x1, x2, W2, b2, z, grad_out,
                 load_x2(s + 6)
             if 1 <= s <= 8:
                 dd_evac(s - 1)
-            if 7 <= s <= 14:
-                scp(s - 7, 1)
             if s + 1 < 8:
                 dzi_qh_qd(s + 1)
             if s < 8:
@@ -390,9 +390,8 @@ def tile_differentiablelogicmachine_pa_v_kernel(tc, x1, x2, W2, b2, z, grad_out,
                 x2si(c)
                 if c + 12 < 16:
                     load_x2(c + 12)
-                scp(c, 0)
+                s_codes(c)
                 q_h(8 + c)
-                qs(c)
             if s < 8:
                 dd(s)
                 if s + 1 < 8:

@@ -1,7 +1,7 @@
 from contextlib import ExitStack
 
 import concourse.mybir as mybir
-from concourse.masks import make_identity
+from concourse.masks import make_block_diagonal, make_identity
 
 F32 = mybir.dt.float32
 BF16 = mybir.dt.bfloat16
@@ -28,9 +28,9 @@ def tile_differentiablelogicmachine_pa_v_kernel(tc, x1, x2, W2, b2, z, grad_out,
     g_v = grad_out.rearrange("b (m e) (k j) o -> m e b k (j o)", e=2, j=2)
     x2_v = x2.rearrange("b (m e) (k j) o -> m e b k (j o)", e=2, j=2)
     x2s_v = x2.rearrange("b (k j) i c -> (b k) j i c", j=2)
-    x1a_v = x1.rearrange("b (q v) c -> q v b c", v=8)
+    x1a_v = x1.rearrange("b (q v) c -> q b v c", v=8)
     x1b_v = x1.rearrange("b (k j) c -> j (b k) c", j=2)
-    out0_v = out_0.rearrange("b i (h j) c -> i h j b c", j=8)
+    out0_v = out_0.rearrange("(g b) i j c -> g i j b c", g=2)
 
     with ExitStack() as ctx:
         const = ctx.enter_context(tc.tile_pool(name="const", bufs=1))
@@ -51,7 +51,6 @@ def tile_differentiablelogicmachine_pa_v_kernel(tc, x1, x2, W2, b2, z, grad_out,
         x1ar = const.tile([P, 2, W], BF16, name="x1ar", tag="x1ar")
         x1br = const.tile([P, 2, W], BF16, name="x1br", tag="x1br")
         wraw = const.tile([P, 8, W], BF16, name="wraw", tag="wraw")
-        vgrp = const.tile([P, 4096], BF16, name="vgrp", tag="vgrp", align_bytes=64)
         vq = const.tile([P, 1024], U32, name="vq", tag="vq", align_bytes=64)
         vs = const.tile([P, 1024], U8, name="vs", tag="vs", align_bytes=64)
         dzq = const.tile([P, NPASS, W], U32, name="dzq", tag="dzq", align_bytes=64)
@@ -60,16 +59,26 @@ def tile_differentiablelogicmachine_pa_v_kernel(tc, x1, x2, W2, b2, z, grad_out,
         dzb = const.tile([P, NPASS, 4, W], BF16, name="dzb", tag="dzb")
         p_b = const.tile([P, 2, W], F32, name="p_b", tag="p_b")
         s_a = const.tile([P, 2, W], F32, name="s_a", tag="s_a")
-        sat = const.tile([P, 4, 16, 16], F32, name="sat", tag="sat")
+        bm = const.tile([P, P], F32, name="bm", tag="bm")
+        cio = const.tile([P, P], F32, name="cio", tag="cio")
+        sel_a = const.tile([P, 8, P], F32, name="sel_a", tag="sel_a")
         sbt = const.tile([P, 2, 4, P], F32, name="sbt", tag="sbt")
         warm = const.tile([P, 1], F32, name="warm", tag="warm")
 
         nc.vector.memset(warm[:], 0.0)
         nc.scalar.activation(out=warm[:], in_=warm[:], func=ACT.Sigmoid)
         make_identity(nc, ident[:])
+        make_block_diagonal(nc, bm[:], 8)
+        nc.gpsimd.iota(
+            cio[:], pattern=[[0, 16], [1, 8]], base=0, channel_multiplier=0, allow_small_or_imprecise_dtypes=True
+        )
+        for v in range(8):
+            nc.vector.scalar_tensor_tensor(
+                out=sel_a[:, v, :], in0=cio[:], scalar=float(v), in1=bm[:], op0=ALU.is_equal, op1=ALU.mult
+            )
 
         nw = nst[:].bitcast(F32)
-        n_v = nw.rearrange("p (i k j b u) -> p i j k b u", i=16, k=8, j=2, b=16, u=2)
+        n_v = nw.rearrange("p (g i k j b u) -> p i j g k b u", g=2, i=16, k=8, j=2, b=8, u=2)
         dzw = dzb[:].bitcast(F32)
 
         ctx.enter_context(tc.manual_schedule())
@@ -100,7 +109,8 @@ def tile_differentiablelogicmachine_pa_v_kernel(tc, x1, x2, W2, b2, z, grad_out,
         zts = {}
         gts = {}
         tpss = {}
-        accas = {}
+        pas = {}
+        sa_ps = {}
         grps = {}
         hqs = {}
 
@@ -162,44 +172,39 @@ def tile_differentiablelogicmachine_pa_v_kernel(tc, x1, x2, W2, b2, z, grad_out,
                     for u in (0, 1):
                         nc.tensor.transpose(tps[:, 2 * jl + u, :], dzw[:, m, 2 * e + jl, u:256:2], ident[:])
                 tpss[h] = tps
-                acc_a = bank(3 + e)
                 for jl in (0, 1):
                     for fc in range(4):
-                        blk = zts[m][:, 2 * e + jl, P * fc : P * (fc + 1)]
                         nc.tensor.matmul(
-                            out=acc_a[:, fc, :], lhsT=blk, rhs=ident[:], is_transpose=True,
-                            start=(jl == 0 and fc == 0), stop=(jl == 1 and fc == 3),
+                            out=acc_b[jl][:, fc, :], lhsT=zts[m][:, 2 * e + jl, P * fc : P * (fc + 1)], rhs=ident[:],
+                            is_transpose=True, start=(h == 0 and fc == 0), stop=(h == 15 and fc == 3),
                         )
-                        nc.tensor.matmul(
-                            out=acc_b[jl][:, fc, :], lhsT=blk, rhs=ident[:], is_transpose=True,
-                            start=(h == 0 and fc == 0), stop=(h == 15 and fc == 3),
-                        )
-                accas[h] = acc_a
+
+            def padd(h):
+                pa = zp.tile([P, W], F32, name="pa", tag="pa", bufs=3)
+                nc.vector.tensor_tensor(
+                    out=pa[:], in0=zts[h // 2][:, 2 * (h % 2), :], in1=zts[h // 2][:, 2 * (h % 2) + 1, :], op=ALU.add
+                )
+                pas[h] = pa
+
+            def sel(h):
+                if h % 8 == 0:
+                    sa_ps[h // 8] = bank(3 + h // 8)
+                nc.tensor.matmul(
+                    out=flat(sa_ps[h // 8]), lhsT=sel_a[:, h % 8, :], rhs=pas[h][:], start=(h % 8 == 0), stop=(h % 8 == 7)
+                )
 
             def evac_n(h):
                 for jl in (0, 1):
-                    dst = n_v[:, h, jl]
-                    src = tpss[h][:, 2 * jl : 2 * jl + 2, :].rearrange("p u (b k) -> p k b u", k=8)
-                    if h % 2 == 0:
-                        nc.scalar.copy(out=dst, in_=src)
-                    else:
-                        nc.vector.tensor_copy(out=dst, in_=src)
-
-            def red(h):
-                nc.vector.tensor_reduce(
-                    out=sat[:, :, h, :],
-                    in_=accas[h][:].rearrange("p f (b k) -> p f b k", k=8),
-                    axis=AX.X, op=ALU.add,
-                )
+                    for g in (0, 1):
+                        dst = n_v[:, h, jl, g]
+                        src = tpss[h][:, 2 * jl : 2 * jl + 2, 64 * g : 64 * (g + 1)].rearrange("p u (b k) -> p k b u", k=8)
+                        if h % 2 == 0:
+                            nc.scalar.copy(out=dst, in_=src)
+                        else:
+                            nc.vector.tensor_copy(out=dst, in_=src)
 
             for m in range(4):
                 load_zg(m)
-            bk_a0 = None
-            heat = bank(7)
-            for n in range(7):
-                nc.tensor.matmul(
-                    out=flat(heat), lhsT=gts[0][:, 0, 0:P], rhs=gts[0][:, 0, :], start=True, stop=True
-                )
             for it in range(19):
                 if it < 16:
                     s12(it)
@@ -208,13 +213,13 @@ def tile_differentiablelogicmachine_pa_v_kernel(tc, x1, x2, W2, b2, z, grad_out,
                 if 3 <= it and (it - 3) % 2 == 0:
                     evac_n(it - 3)
                 if it == 12:
-                    nc.scalar.copy(out=s_a[:, 0, :], in_=flat(bk_a0))
+                    nc.scalar.copy(out=s_a[:, 0, :], in_=flat(sa_ps[0]))
                 if it == 17:
                     x2i(1)
                 if 1 <= it <= 16:
                     v1(it - 1)
-                if 3 <= it:
-                    red(it - 3)
+                if 2 <= it <= 17:
+                    padd(it - 2)
                 if 1 <= it <= 16:
                     cast(it - 1)
                 if 3 <= it and (it - 3) % 2 == 1:
@@ -223,8 +228,8 @@ def tile_differentiablelogicmachine_pa_v_kernel(tc, x1, x2, W2, b2, z, grad_out,
                     dzi_qh_qd(0)
                 if 2 <= it <= 17:
                     pe1(it - 2)
-                if it == 11:
-                    bk_a0 = back_t([sat[:, fc, 0:8, :].rearrange("p v b -> p (v b)") for fc in range(4)], 7)
+                if 3 <= it:
+                    sel(it - 3)
                 if it % 2 == 1 and 3 <= it <= 9:
                     load_zg((it - 3) // 2 + 4)
                 if it == 9:
@@ -240,12 +245,12 @@ def tile_differentiablelogicmachine_pa_v_kernel(tc, x1, x2, W2, b2, z, grad_out,
                         )
 
         late = ctx.enter_context(tc.tile_pool(name="late", bufs=2))
-        ostp = ctx.enter_context(tc.tile_pool(name="ostp", bufs=4))
+        ostp = ctx.enter_context(tc.tile_pool(name="ostp", bufs=8))
         nqa = late.tile([P, 8, W], U32, name="nqa", tag="nqa", bufs=1, align_bytes=64)
         nqsa = late.tile([P, 8, W], U8, name="nqsa", tag="nqsa", bufs=1, align_bytes=64)
-        nc.vector.memset(nqsa[:].rearrange("p c w -> p (c w)").bitcast(I32), 0)
-        n_codes = nqa[:].rearrange("p c w -> p (c w)").bitcast(I32).rearrange("p (x y b) -> p y x b", x=16, y=16)
-        n_scales = nqsa[:].rearrange("p c w -> p (c w)").bitcast(I32).rearrange("p (x y b) -> p y x b", x=16, y=16)
+        vgrp = late.tile([P, 4096], BF16, name="vgrp", tag="vgrp", bufs=1, align_bytes=64)
+        n_codes = nqa[:].rearrange("p c w -> p (c w)").bitcast(I32).rearrange("p (g x y b) -> p g y x b", g=2, x=16, y=16)
+        n_scales = nqsa[:].rearrange("p c w -> p (c w)").bitcast(I32).rearrange("p (g x y b) -> p g y x b", g=2, x=16, y=16)
         sqs = {}
         dds = {}
         vpss = {}
@@ -276,12 +281,12 @@ def tile_differentiablelogicmachine_pa_v_kernel(tc, x1, x2, W2, b2, z, grad_out,
             sq = cdp.tile([P, W], U32, name="sq", tag="sq", align_bytes=64)
             sqsc = cdp.tile([P, W], U8, name="sqsc", tag="sqsc", align_bytes=64)
             nc.vector.tensor_copy(
-                out=sq[:].bitcast(I32).rearrange("p (y x b) -> p y x b", y=2, x=16),
-                in_=n_codes[:, 2 * c : 2 * c + 2],
+                out=sq[:].bitcast(I32).rearrange("p (y x b) -> p y x b", y=4, x=16),
+                in_=n_codes[:, c // 4, 4 * (c % 4) : 4 * (c % 4) + 4],
             )
             nc.vector.tensor_copy(
-                out=sqsc[:].bitcast(I32).rearrange("p (y x b) -> p y x b", y=2, x=16),
-                in_=n_scales[:, 2 * c : 2 * c + 2],
+                out=sqsc[:].bitcast(I32).rearrange("p (y x b) -> p y x b", y=4, x=16),
+                in_=n_scales[:, c // 4, 4 * (c % 4) : 4 * (c % 4) + 4],
             )
             sqs[c] = (sq, sqsc)
 
@@ -304,7 +309,7 @@ def tile_differentiablelogicmachine_pa_v_kernel(tc, x1, x2, W2, b2, z, grad_out,
 
         def dd(n):
             cc = n % 4
-            acc = bank(6 if n % 2 == 0 else 0)
+            acc = bank(6 if n % 2 == 0 else 4)
             lhs = x1a if n < 4 else x1b
             rhs = s_a if n < 4 else p_b
             for q in (0, 1):
@@ -320,7 +325,7 @@ def tile_differentiablelogicmachine_pa_v_kernel(tc, x1, x2, W2, b2, z, grad_out,
             nc.sync.dma_start(out=out_1[r0 : r0 + P, :], in_=o1[:])
 
         def vprep_t(a2):
-            vps = bank(4 + a2 % 2)
+            vps = bank(0 if a2 % 2 == 0 else 5)
             for a in (0, 1):
                 words = wraw[:, 2 * a2 + a, :].bitcast(F32)
                 for u in (0, 1):
@@ -351,7 +356,7 @@ def tile_differentiablelogicmachine_pa_v_kernel(tc, x1, x2, W2, b2, z, grad_out,
         def p_evac(c, a):
             ost = ostp.tile([P, W], F32, name="ost", tag="ost")
             negate_out(a % 2 if c == 7 else 0, ost[:], flat(paccs[(c, a)]))
-            nc.sync.dma_start(out=out0_v[2 * c + a // 2, a % 2], in_=ost[:])
+            nc.sync.dma_start(out=out0_v[c // 4, 4 * (c % 4) + a], in_=ost[:])
 
         load_x2(4)
         load_x2(5)
@@ -361,10 +366,9 @@ def tile_differentiablelogicmachine_pa_v_kernel(tc, x1, x2, W2, b2, z, grad_out,
             nc.scalar.copy(out=sbt[:, jl, :, :], in_=acc_b[jl][:])
         maccs = [bank(n) for n in m_banks]
         m_step(maccs, 0)
-        bk_b0 = back_t([sbt[:, 0, fc, :] for fc in range(4)], 4)
+        bk_b0 = back_t([sbt[:, 0, fc, :] for fc in range(4)], 0)
         bk_b1 = back_t([sbt[:, 1, fc, :] for fc in range(4)], 5)
-        bk_a1 = back_t([sat[:, fc, 8:16, :].rearrange("p v b -> p (v b)") for fc in range(4)], 0)
-        nc.scalar.copy(out=s_a[:, 1, :], in_=flat(bk_a1))
+        nc.scalar.copy(out=s_a[:, 1, :], in_=flat(sa_ps[1]))
         nc.scalar.copy(out=p_b[:, 0, :], in_=flat(bk_b0))
         nc.scalar.copy(out=p_b[:, 1, :], in_=flat(bk_b1))
 
@@ -376,6 +380,8 @@ def tile_differentiablelogicmachine_pa_v_kernel(tc, x1, x2, W2, b2, z, grad_out,
                 dd_evac(s - 1)
             if s + 1 < 8:
                 dzi_qh_qd(s + 1)
+            if s == 0:
+                nc.vector.memset(nqsa[:].rearrange("p c w -> p (c w)").bitcast(I32), 0)
             if s < 8:
                 qn(s)
             if 2 <= s <= 5:

@@ -150,9 +150,12 @@ def tile_differentiablelogicmachine_pa_v_kernel(tc, x1, x2, W2, b2, z, grad_out,
             def half(t, h):
                 return t[h // 2][:, 2 * (h % 2) : 2 * (h % 2) + 2, :]
 
-            def s12(h):
+            def s1(h):
                 ze = half(zts, h)
                 nc.scalar.activation(out=ze, in_=ze, func=ACT.Sigmoid)
+
+            def s2(h):
+                ze = half(zts, h)
                 nc.scalar.activation(out=ze, in_=ze, func=ACT.Square, bias=-0.5)
 
             def v1(h):
@@ -198,19 +201,24 @@ def tile_differentiablelogicmachine_pa_v_kernel(tc, x1, x2, W2, b2, z, grad_out,
                     for g in (0, 1):
                         dst = n_v[:, h, jl, g]
                         src = tpss[h][:, 2 * jl : 2 * jl + 2, 64 * g : 64 * (g + 1)].rearrange("p u (b k) -> p k b u", k=8)
-                        if h % 2 == 0:
+                        if h % 4 == 0:
                             nc.scalar.copy(out=dst, in_=src)
                         else:
                             nc.vector.tensor_copy(out=dst, in_=src)
 
             for m in range(4):
                 load_zg(m)
+            s1(0)
             for it in range(19):
-                if it < 16:
-                    s12(it)
+                if it == 0:
+                    s2(0)
+                if it + 1 < 16:
+                    s1(it + 1)
+                if 1 <= it < 16:
+                    s2(it)
                 if it == 16:
                     x2i(0)
-                if 3 <= it and (it - 3) % 2 == 0:
+                if 3 <= it and (it - 3) % 4 == 0:
                     evac_n(it - 3)
                 if it == 12:
                     nc.scalar.copy(out=s_a[:, 0, :], in_=flat(sa_ps[0]))
@@ -222,7 +230,7 @@ def tile_differentiablelogicmachine_pa_v_kernel(tc, x1, x2, W2, b2, z, grad_out,
                     padd(it - 2)
                 if 1 <= it <= 16:
                     cast(it - 1)
-                if 3 <= it and (it - 3) % 2 == 1:
+                if 3 <= it and (it - 3) % 4 != 0:
                     evac_n(it - 3)
                 if it == 17:
                     dzi_qh_qd(0)

from contextlib import ExitStack

import concourse.mybir as mybir
from concourse.masks import make_block_diagonal, make_identity

F32 = mybir.dt.float32
BF16 = mybir.dt.bfloat16
U32 = mybir.dt.uint32
U8 = mybir.dt.uint8
I32 = mybir.dt.int32
E4 = mybir.dt.float8_e4m3fn_x4
E5 = mybir.dt.float8_e5m2_x4
ACT = mybir.ActivationFunctionType
ALU = mybir.AluOpType
AX = mybir.AxisListType

FLOPS = 2 * (2 * 4096 * 512 * 1024) + 2 * (2 * 256 * 512 * 512)

P = 128
W = 512
NPASS = 8


def tile_differentiablelogicmachine_pa_v_kernel(tc, x1, x2, W2, b2, z, grad_out, out_0, out_1):
    nc = tc.nc

    z_v = z.rearrange("b (m e) (k j) o -> m e b k (j o)", e=2, j=2)
    g_v = grad_out.rearrange("b (m e) (k j) o -> m e b k (j o)", e=2, j=2)
    x2_v = x2.rearrange("b (m e) (k j) o -> m e b k (j o)", e=2, j=2)
    x2s_v = x2.rearrange("b (k j) i c -> (b k) j i c", j=2)
    x1a_v = x1.rearrange("b (q v) c -> q b v c", v=8)
    x1b_v = x1.rearrange("b (k j) c -> j (b k) c", j=2)
    out0_v = out_0.rearrange("(g b) i j c -> g i j b c", g=2)

    with ExitStack() as ctx:
        const = ctx.enter_context(tc.tile_pool(name="const", bufs=1))
        psum = ctx.enter_context(tc.psum_pool(name="psum", bufs=1))
        grpp = ctx.enter_context(tc.tile_pool(name="grpp", bufs=2))
        cdp = ctx.enter_context(tc.tile_pool(name="cdp", bufs=3))
        x2p = ctx.enter_context(tc.tile_pool(name="x2p", bufs=4))

        def bank(n):
            return psum.tile([P, 4, P], F32, name="bank%d" % n, tag="bank%d" % n)

        def flat(t):
            return t[:].rearrange("p f r -> p (f r)")

        ident = const.tile([P, P], F32, name="ident", tag="ident")
        x1a = const.tile([P, 2, W], F32, name="x1a", tag="x1a")
        x1b = const.tile([P, 2, W], F32, name="x1b", tag="x1b")
        x1ar = const.tile([P, 2, W], BF16, name="x1ar", tag="x1ar")
        x1br = const.tile([P, 2, W], BF16, name="x1br", tag="x1br")
        wraw = const.tile([P, 8, W], BF16, name="wraw", tag="wraw")
        vq = const.tile([P, 1024], U32, name="vq", tag="vq", align_bytes=64)
        vs = const.tile([P, 1024], U8, name="vs", tag="vs", align_bytes=64)
        dzq = const.tile([P, NPASS, W], U32, name="dzq", tag="dzq", align_bytes=64)
        dzs = const.tile([P, NPASS, W], U8, name="dzs", tag="dzs", align_bytes=64)
        nst = const.tile([P, 4096 * 4], BF16, name="nst", tag="nst", align_bytes=64)
        dzb = const.tile([P, NPASS, 4, W], BF16, name="dzb", tag="dzb")
        p_b = const.tile([P, 2, W], F32, name="p_b", tag="p_b")
        s_a = const.tile([P, 2, W], F32, name="s_a", tag="s_a")
        bm = const.tile([P, P], F32, name="bm", tag="bm")
        cio = const.tile([P, P], F32, name="cio", tag="cio")
        sel_a = const.tile([P, 8, P], F32, name="sel_a", tag="sel_a")
        sbt = const.tile([P, 2, 4, P], F32, name="sbt", tag="sbt")
        warm = const.tile([P, 1], F32, name="warm", tag="warm")

        nc.vector.memset(warm[:], 0.0)
        nc.scalar.activation(out=warm[:], in_=warm[:], func=ACT.Sigmoid)
        make_identity(nc, ident[:])
        make_block_diagonal(nc, bm[:], 8)
        nc.gpsimd.iota(
            cio[:], pattern=[[0, 16], [1, 8]], base=0, channel_multiplier=0, allow_small_or_imprecise_dtypes=True
        )
        for v in range(8):
            nc.vector.scalar_tensor_tensor(
                out=sel_a[:, v, :], in0=cio[:], scalar=float(v), in1=bm[:], op0=ALU.is_equal, op1=ALU.mult
            )

        nw = nst[:].bitcast(F32)
        n_v = nw.rearrange("p (g i k j b u) -> p i j g k b u", g=2, i=16, k=8, j=2, b=8, u=2)
        dzw = dzb[:].bitcast(F32)

        ctx.enter_context(tc.manual_schedule())

        x2ts = {}

        def load_x2(n):
            x2t = x2p.tile([P, 4, W], BF16, name="x2t", tag="x2t")
            if n < 8:
                for e in (0, 1):
                    nc.sync.dma_start(
                        out=x2t[:, 2 * e : 2 * e + 2, :].rearrange("p t o -> p (t o)"), in_=x2_v[n, e]
                    )
            else:
                i0 = 2 * (n - 8)
                nc.sync.dma_start(
                    out=x2t[:].rearrange("p (j e) c -> p j e c", e=2), in_=x2s_v[:, :, i0 : i0 + 2, :]
                )
            x2ts[n] = x2t

        def back_t(src, n):
            bk = bank(n)
            for fc in range(4):
                nc.tensor.transpose(bk[:, fc, :], src[fc], ident[:])
            return bk

        acc_b = [bank(5), bank(6)]
        zts = {}
        gts = {}
        tpss = {}
        pas = {}
        sa_ps = {}
        grps = {}
        hqs = {}

        def x2i(s):
            grp = grpp.tile([P, W, 4], BF16, name="grph", tag="grph", bufs=3, align_bytes=64)
            nc.scalar.copy(out=grp[:], in_=x2ts[s][:].rearrange("p t o -> p o t"))
            grps[s] = grp

        def dzi_qh_qd(s):
            grd = grpp.tile([P, W, 4], BF16, name="grpd", tag="grpd", align_bytes=64)
            nc.vector.tensor_copy(out=grd[:], in_=dzb[:, s, :, :].rearrange("p t o -> p o t"))
            q_h(s)
            nc.vector.quantize_mx(
                out=dzq[:, s, :].bitcast(E5), scales=dzs[:, s, :], in_=grd[:].rearrange("p o t -> p (o t)")
            )

        def q_h(s):
            hq = cdp.tile([P, W], U32, name="hq", tag="hq", align_bytes=64)
            hs = cdp.tile([P, W], U8, name="hs", tag="hs", align_bytes=64)
            nc.vector.quantize_mx(
                out=hq[:].bitcast(E4), scales=hs[:], in_=grps[s][:].rearrange("p o t -> p (o t)")
            )
            hqs[s] = (hq, hs)

        with tc.tile_pool(name="zp", bufs=4) as zp:

            def load_zg(m):
                zt = zp.tile([P, 4, W], F32, name="zt", tag="zt")
                gt = zp.tile([P, 4, W], BF16, name="gt", tag="gt")
                for e in (0, 1):
                    sl = slice(2 * e, 2 * e + 2)
                    nc.sync.dma_start(out=zt[:, sl, :].rearrange("p t o -> p (t o)"), in_=z_v[m, e])
                    nc.sync.dma_start(out=gt[:, sl, :].rearrange("p t o -> p (t o)"), in_=g_v[m, e])
                zts[m] = zt
                gts[m] = gt

            def half(t, h):
                return t[h // 2][:, 2 * (h % 2) : 2 * (h % 2) + 2, :]

            def s1(h):
                ze = half(zts, h)
                nc.scalar.activation(out=ze, in_=ze, func=ACT.Sigmoid)

            def s2(h):
                ze = half(zts, h)
                nc.scalar.activation(out=ze, in_=ze, func=ACT.Square, bias=-0.5)

            def v1(h):
                ze = half(zts, h)
                nc.vector.scalar_tensor_tensor(
                    out=ze, in0=ze, scalar=0.25, in1=half(gts, h), op0=ALU.subtract, op1=ALU.mult
                )

            def cast(h):
                nc.vector.tensor_copy(out=dzb[:, h // 2, 2 * (h % 2) : 2 * (h % 2) + 2, :], in_=half(zts, h))

            def pe1(h):
                m = h // 2
                e = h % 2
                tps = bank(h % 3)
                for jl in (0, 1):
                    for u in (0, 1):
                        nc.tensor.transpose(tps[:, 2 * jl + u, :], dzw[:, m, 2 * e + jl, u:256:2], ident[:])
                tpss[h] = tps
                for jl in (0, 1):
                    for fc in range(4):
                        nc.tensor.matmul(
                            out=acc_b[jl][:, fc, :], lhsT=zts[m][:, 2 * e + jl, P * fc : P * (fc + 1)], rhs=ident[:],
                            is_transpose=True, start=(h == 0 and fc == 0), stop=(h == 15 and fc == 3),
                        )

            def padd(h):
                pa = zp.tile([P, W], F32, name="pa", tag="pa", bufs=3)
                nc.vector.tensor_tensor(
                    out=pa[:], in0=zts[h // 2][:, 2 * (h % 2), :], in1=zts[h // 2][:, 2 * (h % 2) + 1, :], op=ALU.add
                )
                pas[h] = pa

            def sel(h):
                if h % 8 == 0:
                    sa_ps[h // 8] = bank(3 + h // 8)
                nc.tensor.matmul(
                    out=flat(sa_ps[h // 8]), lhsT=sel_a[:, h % 8, :], rhs=pas[h][:], start=(h % 8 == 0), stop=(h % 8 == 7)
                )

            def evac_n(h):
                for jl in (0, 1):
                    for g in (0, 1):
                        dst = n_v[:, h, jl, g]
                        src = tpss[h][:, 2 * jl : 2 * jl + 2, 64 * g : 64 * (g + 1)].rearrange("p u (b k) -> p k b u", k=8)
                        if h % 4 == 0:
                            nc.scalar.copy(out=dst, in_=src)
                        else:
                            nc.vector.tensor_copy(out=dst, in_=src)

            for m in range(4):
                load_zg(m)
            s1(0)
            for it in range(19):
                if it == 0:
                    s2(0)
                if it + 1 < 16:
                    s1(it + 1)
                if 1 <= it < 16:
                    s2(it)
                if it == 16:
                    x2i(0)
                if 3 <= it and (it - 3) % 4 == 0:
                    evac_n(it - 3)
                if it == 12:
                    nc.scalar.copy(out=s_a[:, 0, :], in_=flat(sa_ps[0]))
                if it == 17:
                    x2i(1)
                if 1 <= it <= 16:
                    v1(it - 1)
                if 2 <= it <= 17:
                    padd(it - 2)
                if 1 <= it <= 16:
                    cast(it - 1)
                if 3 <= it and (it - 3) % 4 != 0:
                    evac_n(it - 3)
                if it == 17:
                    dzi_qh_qd(0)
                if 2 <= it <= 17:
                    pe1(it - 2)
                if 3 <= it:
                    sel(it - 3)
                if it % 2 == 1 and 3 <= it <= 9:
                    load_zg((it - 3) // 2 + 4)
                if it == 9:
                    for q in (0, 1):
                        nc.sync.dma_start(out=x1ar[:, q, :], in_=x1a_v[q])
                        nc.sync.dma_start(out=x1br[:, q, :], in_=x1b_v[q])
                    for n in range(4):
                        load_x2(n)
                    for s in (0, 1):
                        nc.sync.dma_start(
                            out=wraw[:, 4 * s : 4 * s + 4, :],
                            in_=W2[512 + 1024 * s : 1024 + 1024 * s, :].rearrange("(r p) o -> p r o", p=P),
                        )

        late = ctx.enter_context(tc.tile_pool(name="late", bufs=2))
        ostp = ctx.enter_context(tc.tile_pool(name="ostp", bufs=8))
        nqa = late.tile([P, 8, W], U32, name="nqa", tag="nqa", bufs=1, align_bytes=64)
        nqsa = late.tile([P, 8, W], U8, name="nqsa", tag="nqsa", bufs=1, align_bytes=64)
        vgrp = late.tile([P, 4096], BF16, name="vgrp", tag="vgrp", bufs=1, align_bytes=64)
        n_codes = nqa[:].rearrange("p c w -> p (c w)").bitcast(I32).rearrange("p (g x y b) -> p g y x b", g=2, x=16, y=16)
        n_scales = nqsa[:].rearrange("p c w -> p (c w)").bitcast(I32).rearrange("p (g x y b) -> p g y x b", g=2, x=16, y=16)
        sqs = {}
        dds = {}
        vpss = {}
        paccs = {}
        m_banks = (7, 1, 3, 2)
        p_banks = (4, 5, 6, 0)

        def negate_out(eng, out, in_):
            if eng == 0:
                nc.scalar.activation(out=out, in_=in_, func=ACT.Copy, scale=-1.0)
            else:
                nc.vector.tensor_scalar(out=out, in0=in_, scalar1=-1.0, scalar2=None, op0=ALU.mult)

        def qn(c):
            nc.vector.quantize_mx(
                out=nqa[:, c, :].bitcast(E5), scales=nqsa[:, c, :], in_=nst[:, 2048 * c : 2048 * (c + 1)]
            )

        def x2si(c):
            grp = grpp.tile([P, W, 4], BF16, name="grph", tag="grph", bufs=3, align_bytes=64)
            nc.vector.tensor_copy(
                out=grp[:].rearrange("p c (e j) -> p c e j", j=2),
                in_=x2ts[8 + c][:].rearrange("p (j e) c -> p c e j", e=2),
            )
            grps[8 + c] = grp

        def s_codes(c):
            sq = cdp.tile([P, W], U32, name="sq", tag="sq", align_bytes=64)
            sqsc = cdp.tile([P, W], U8, name="sqsc", tag="sqsc", align_bytes=64)
            nc.vector.tensor_copy(
                out=sq[:].bitcast(I32).rearrange("p (y x b) -> p y x b", y=4, x=16),
                in_=n_codes[:, c // 4, 4 * (c % 4) : 4 * (c % 4) + 4],
            )
            nc.vector.tensor_copy(
                out=sqsc[:].bitcast(I32).rearrange("p (y x b) -> p y x b", y=4, x=16),
                in_=n_scales[:, c // 4, 4 * (c % 4) : 4 * (c % 4) + 4],
            )
            sqs[c] = (sq, sqsc)

        def m_step(maccs, s):
            hq, hs = hqs[s]
            m = s % 8
            for a in range(4):
                cols = slice(P * a, P * (a + 1))
                nc.tensor.matmul_mx(
                    out=flat(maccs[a]), lhsT=hq[:, cols].bitcast(E4), lhsT_scale=hs[:, cols],
                    rhs=dzq[:, m, :].bitcast(E5), rhs_scale=dzs[:, m, :],
                    start=(m == 0), stop=(m == NPASS - 1),
                )

        def m_evac(maccs, sweep, a):
            o1 = late.tile([P, W], F32, name="o1", tag="o1", bufs=3)
            negate_out(a % 2, o1[:], flat(maccs[a]))
            r0 = 512 + 1024 * sweep + P * a
            nc.sync.dma_start(out=out_1[r0 : r0 + P, :], in_=o1[:])

        def dd(n):
            cc = n % 4
            acc = bank(6 if n % 2 == 0 else 4)
            lhs = x1a if n < 4 else x1b
            rhs = s_a if n < 4 else p_b
            for q in (0, 1):
                nc.tensor.matmul(
                    out=flat(acc), lhsT=lhs[:, q, P * cc : P * (cc + 1)], rhs=rhs[:, q, :], start=(q == 0), stop=(q == 1)
                )
            dds[n] = acc

        def dd_evac(n):
            o1 = late.tile([P, W], F32, name="o1", tag="o1", bufs=3)
            negate_out(0, o1[:], flat(dds[n]))
            r0 = P * (n % 4) + (0 if n < 4 else 1024)
            nc.sync.dma_start(out=out_1[r0 : r0 + P, :], in_=o1[:])

        def vprep_t(a2):
            vps = bank(0 if a2 % 2 == 0 else 5)
            for a in (0, 1):
                words = wraw[:, 2 * a2 + a, :].bitcast(F32)
                for u in (0, 1):
                    nc.tensor.transpose(vps[:, 2 * a + u, :], words[:, u:256:2], ident[:])
            vpss[a2] = vps

        def vprep_e(a2):
            nc.vector.tensor_copy(
                out=vgrp[:].bitcast(F32)[:, 512 * a2 : 512 * (a2 + 1)].rearrange("p (a r u) -> p a r u", a=2, u=2),
                in_=vpss[a2][:].rearrange("p (a u) r -> p a r u", u=2),
            )

        def p_mm(c):
            sq, sqsc = sqs[c]
            for a in range(4):
                cols = slice(P * a, P * (a + 1))
                acc = bank(p_banks[a])
                nc.tensor.matmul_mx(
                    out=flat(acc), lhsT=nqa[:, c, cols].bitcast(E5), lhsT_scale=nqsa[:, c, cols],
                    rhs=vq[:, 0:512].bitcast(E4), rhs_scale=vs[:, 0:512], start=True, stop=False,
                )
                nc.tensor.matmul_mx(
                    out=flat(acc), lhsT=sq[:, cols].bitcast(E5), lhsT_scale=sqsc[:, cols],
                    rhs=vq[:, 512:1024].bitcast(E4), rhs_scale=vs[:, 512:1024], start=False, stop=True,
                )
                paccs[(c, a)] = acc

        def p_evac(c, a):
            ost = ostp.tile([P, W], F32, name="ost", tag="ost")
            negate_out(a % 2 if c == 7 else 0, ost[:], flat(paccs[(c, a)]))
            nc.sync.dma_start(out=out0_v[c // 4, 4 * (c % 4) + a], in_=ost[:])

        load_x2(4)
        load_x2(5)
        nc.vector.tensor_copy(out=x1a[:], in_=x1ar[:])
        nc.vector.tensor_copy(out=x1b[:], in_=x1br[:])
        for jl in (0, 1):
            nc.scalar.copy(out=sbt[:, jl, :, :], in_=acc_b[jl][:])
        maccs = [bank(n) for n in m_banks]
        m_step(maccs, 0)
        bk_b0 = back_t([sbt[:, 0, fc, :] for fc in range(4)], 0)
        bk_b1 = back_t([sbt[:, 1, fc, :] for fc in range(4)], 5)
        nc.scalar.copy(out=s_a[:, 1, :], in_=flat(sa_ps[1]))
        nc.scalar.copy(out=p_b[:, 0, :], in_=flat(bk_b0))
        nc.scalar.copy(out=p_b[:, 1, :], in_=flat(bk_b1))

        for s in range(16):
            if s + 2 < 8:
                x2i(s + 2)
                load_x2(s + 6)
            if 1 <= s <= 8:
                dd_evac(s - 1)
            if s + 1 < 8:
                dzi_qh_qd(s + 1)
            if s == 0:
                nc.vector.memset(nqsa[:].rearrange("p c w -> p (c w)").bitcast(I32), 0)
            if s < 8:
                qn(s)
            if 2 <= s <= 5:
                vprep_e(s - 2)
            if s == 6:
                nc.vector.quantize_mx(out=vq[:].bitcast(E4), scales=vs[:], in_=vgrp[:])
            if s == 7:
                for a in range(4):
                    m_evac(maccs, 0, a)
            if 7 <= s <= 14:
                c = s - 7
                x2si(c)
                if c + 12 < 16:
                    load_x2(c + 12)
                s_codes(c)
                q_h(8 + c)
            if s < 8:
                dd(s)
                if s + 1 < 8:
                    m_step(maccs, s + 1)
                if 1 <= s <= 4:
                    vprep_t(s - 1)
            else:
                if s == 8:
                    maccs = [bank(n) for n in m_banks]
                if s < 15:
                    p_mm(s - 8)
                    m_step(maccs, s)
                else:
                    m_step(maccs, s)
                    p_mm(s - 8)
                    for a in range(4):
                        m_evac(maccs, 1, a)
                for a in range(4):
                    p_evac(s - 8, a)
